import numpy as np
import ml_dtypes


def mxq(x, axis, fmt="e4m3"):
    dtype, down = {"e4m3": (ml_dtypes.float8_e4m3fn, 7), "e5m2": (ml_dtypes.float8_e5m2, 14)}[fmt]
    v = np.moveaxis(np.asarray(x, np.float32).astype(ml_dtypes.bfloat16).astype(np.float64), axis, -1)
    blocks = v.reshape(v.shape[:-1] + (-1, 32))
    amax = np.abs(blocks).max(-1, keepdims=True)
    byte = np.maximum(np.where(amax > 0, np.frexp(amax)[1] - 1 + 127, 0) - down, 1)
    scale = np.exp2(byte - 127.0)
    codes = (blocks / scale).astype(np.float32).astype(dtype).astype(np.float64)
    return np.moveaxis((codes * scale).reshape(v.shape), -1, axis)


WIDE = False


def mx_kscale(k):
    if not WIDE:
        return np.ones(k)
    levels = np.array([20, -20, 10, -10, 0])
    a = np.random.permutation(np.resize(levels, k // 512 * 4)).reshape(k // 512, 4)
    idx = np.arange(k)
    return np.exp2(a[idx // 512, idx % 128 // 32])


BF16 = ml_dtypes.bfloat16


def bf(x):
    return np.asarray(x, np.float32).astype(BF16)


def f64(x):
    return np.asarray(x).astype(np.float64)


B, DIM = 4096, 512


def setup_inputs():
    s = mx_kscale(DIM)
    p = np.random.standard_normal((B, DIM)) / s
    q = np.random.standard_normal((B, DIM)) * s
    A = np.random.standard_normal((DIM, DIM)) * 0.7 / np.sqrt(DIM) / s[:, None] / s[None, :]
    g = np.random.standard_normal((B, 2 * DIM)) * np.exp2(np.random.randint(-12, 1, (B, 1))) * 4.0
    g = g * np.concatenate([s, 1.0 / s])[None, :]
    return {"pq": bf(np.concatenate([p, q], axis=1)), "A": bf(A), "grad_out": bf(g)}


def reference(pq, A, grad_out):
    A, g = f64(A), f64(grad_out)
    S = A + A.T
    gp = g[:, :DIM]
    gq = g[:, DIM:]
    qterm = mxq(gp, 1, "e5m2") @ mxq(S, 0, "e4m3")
    return np.concatenate([gp, gq + qterm], axis=-1)

@@ -1,0 +1,136 @@
+from contextlib import ExitStack
+
+import concourse.mybir as mybir
+from concourse.masks import make_identity
+
+BF16 = mybir.dt.bfloat16
+F32 = mybir.dt.float32
+U32 = mybir.dt.uint32
+U8 = mybir.dt.uint8
+E4M3_X4 = mybir.dt.float8_e4m3fn_x4
+E5M2_X4 = mybir.dt.float8_e5m2_x4
+ADD = mybir.AluOpType.add
+
+P = 128
+PACK = 4
+HALVES = 2
+DIM = P * PACK
+TOKENS = 4096
+TILES = TOKENS // P
+PAIR = 2
+ROUND = 4
+ROUNDS = TILES // ROUND
+
+FLOPS = 2 * TOKENS * DIM * DIM
+BYTES = TOKENS * 2 * DIM * 2 + DIM * DIM * 2 + TOKENS * 2 * DIM * 4
+
+
+def transpose_pair(nc, banks, words, ident):
+    flipped = banks.tile([P, PAIR, HALVES, P], F32)
+    for i in range(PAIR):
+        for h in range(HALVES):
+            nc.tensor.transpose(
+                out=flipped[:, i, h, :],
+                in_=words[:, i, h : DIM // 2 : HALVES],
+                identity=ident,
+            )
+    return flipped
+
+
+def tile_linear_sub_t_kernel(tc, pq, A, grad_out, out):
+    nc = tc.nc
+    grad_tiles = grad_out.rearrange("(p t) f -> p t f", t=TILES)
+    out_tiles = out.rearrange("(p t) f -> p t f", t=TILES)
+
+    with ExitStack() as ctx:
+        const = ctx.enter_context(tc.tile_pool(name="const", bufs=1))
+        loaded = ctx.enter_context(tc.tile_pool(name="loaded", bufs=ROUNDS))
+        results = ctx.enter_context(tc.tile_pool(name="results", bufs=ROUNDS))
+        stage = ctx.enter_context(tc.tile_pool(name="stage", bufs=3))
+        banks = ctx.enter_context(tc.psum_pool(name="banks", bufs=4))
+        products = ctx.enter_context(tc.psum_pool(name="products", bufs=4))
+
+        a_rows = const.tile([P, PACK, DIM], BF16)
+        nc.sync.dma_start(out=a_rows[:], in_=A.rearrange("(p j) d -> p j d", j=PACK))
+        grads = []
+        for g in range(ROUNDS):
+            grad = loaded.tile([P, ROUND, 2 * DIM], BF16)
+            nc.sync.dma_start(out=grad[:], in_=grad_tiles[:, g * ROUND : (g + 1) * ROUND, :])
+            grads.append(grad)
+
+        ident = const.tile([P, P], F32)
+        make_identity(nc, ident[:])
+
+        s_grouped = const.tile([P, DIM, PACK], BF16, align_bytes=64)
+        a_words = a_rows[:].bitcast(F32)
+        for b in range(PACK // PAIR):
+            c_range = slice(b * PAIR, (b + 1) * PAIR)
+            flipped = transpose_pair(nc, banks, a_words[:, c_range, :], ident[:])
+            nc.vector.tensor_tensor(
+                out=s_grouped[:].rearrange("p (q c) (h e) -> p q c h e", c=PACK, e=2)[
+                    :, :, c_range
+                ],
+                in0=a_rows[:].rearrange("p (h e) (q c) -> p q c h e", c=PACK, e=2)[
+                    :, :, c_range
+                ],
+                in1=flipped[:].bitcast(BF16).rearrange("p i h (q e) -> p q i h e", e=2),
+                op=ADD,
+            )
+        s_codes = const.tile([P, DIM], U32, align_bytes=64)
+        s_scales = const.tile([P, DIM], U8, align_bytes=64)
+        nc.vector.quantize_mx(
+            out=s_codes[:].bitcast(E4M3_X4),
+            scales=s_scales[:],
+            in_=s_grouped[:].rearrange("p d j -> p (d j)"),
+        )
+
+        def quantise_round(g):
+            grad_words = grads[g][:].bitcast(F32)
+            grouped = stage.tile([P, ROUND, P, PACK], BF16, align_bytes=64)
+            grouped_words = grouped[:].bitcast(F32)
+            for b in range(ROUND // PAIR):
+                pair = slice(b * PAIR, (b + 1) * PAIR)
+                flipped = transpose_pair(nc, banks, grad_words[:, pair, 0 : DIM // 2], ident[:])
+                nc.scalar.copy(
+                    out=grouped_words[:, pair, :, :],
+                    in_=flipped[:].rearrange("p i h r -> p i r h"),
+                )
+            codes = stage.tile([P, ROUND * P], U32, align_bytes=64)
+            scales = stage.tile([P, ROUND * P], U8, align_bytes=64)
+            nc.vector.quantize_mx(
+                out=codes[:].bitcast(E5M2_X4),
+                scales=scales[:],
+                in_=grouped[:].rearrange("p i r j -> p (i r j)"),
+            )
+            return codes, scales
+
+        def finish_round(g, codes, scales):
+            grad = grads[g]
+            result = results.tile([P, ROUND, 2 * DIM], F32)
+            nc.scalar.copy(out=result[:, :, 0:DIM], in_=grad[:, :, 0:DIM])
+            for i in range(ROUND):
+                tokens = slice(i * P, (i + 1) * P)
+                product = products.tile([P, DIM], F32)
+                nc.tensor.matmul_mx(
+                    out=product[:],
+                    lhsT=codes[:, tokens].bitcast(E5M2_X4),
+                    lhsT_scale=scales[:, tokens],
+                    rhs=s_codes[:].bitcast(E4M3_X4),
+                    rhs_scale=s_scales[:],
+                    start=True,
+                    stop=True,
+                )
+                nc.vector.tensor_tensor(
+                    out=result[:, i, DIM : 2 * DIM],
+                    in0=product[:],
+                    in1=grad[:, i, DIM : 2 * DIM],
+                    op=ADD,
+                )
+            nc.sync.dma_start(out=out_tiles[:, g * ROUND : (g + 1) * ROUND, :], in_=result[:])
+
+        ahead = quantise_round(0)
+        for g in range(ROUNDS):
+            codes, scales = ahead
+            if g + 1 < ROUNDS:
+                ahead = quantise_round(g + 1)
+            finish_round(g, codes, scales)

@@ -20,6 +20,8 @@ TILES = TOKENS // P
 PAIR = 2
 ROUND = 4
 ROUNDS = TILES // ROUND
+CHUNK = 8
+CHUNKS = TILES // CHUNK
 
 FLOPS = 2 * TOKENS * DIM * DIM
 BYTES = TOKENS * 2 * DIM * 2 + DIM * DIM * 2 + TOKENS * 2 * DIM * 4
@@ -44,8 +46,8 @@ def tile_linear_sub_t_kernel(tc, pq, A, grad_out, out):
 
     with ExitStack() as ctx:
         const = ctx.enter_context(tc.tile_pool(name="const", bufs=1))
-        loaded = ctx.enter_context(tc.tile_pool(name="loaded", bufs=ROUNDS))
-        results = ctx.enter_context(tc.tile_pool(name="results", bufs=ROUNDS))
+        loaded = ctx.enter_context(tc.tile_pool(name="loaded", bufs=CHUNKS))
+        stored = ctx.enter_context(tc.tile_pool(name="stored", bufs=CHUNKS))
         stage = ctx.enter_context(tc.tile_pool(name="stage", bufs=3))
         banks = ctx.enter_context(tc.psum_pool(name="banks", bufs=4))
         products = ctx.enter_context(tc.psum_pool(name="products", bufs=4))
@@ -53,10 +55,13 @@ def tile_linear_sub_t_kernel(tc, pq, A, grad_out, out):
         a_rows = const.tile([P, PACK, DIM], BF16)
         nc.sync.dma_start(out=a_rows[:], in_=A.rearrange("(p j) d -> p j d", j=PACK))
         grads = []
-        for g in range(ROUNDS):
-            grad = loaded.tile([P, ROUND, 2 * DIM], BF16)
-            nc.sync.dma_start(out=grad[:], in_=grad_tiles[:, g * ROUND : (g + 1) * ROUND, :])
+        results = []
+        for c in range(CHUNKS):
+            grad = loaded.tile([P, CHUNK, 2 * DIM], BF16)
+            nc.sync.dma_start(out=grad[:], in_=grad_tiles[:, c * CHUNK : (c + 1) * CHUNK, :])
             grads.append(grad)
+            result = stored.tile([P, CHUNK, 2 * DIM], F32)
+            results.append(result)
 
         ident = const.tile([P, P], F32)
         make_identity(nc, ident[:])
@@ -85,12 +90,18 @@ def tile_linear_sub_t_kernel(tc, pq, A, grad_out, out):
         )
 
         def quantise_round(g):
-            grad_words = grads[g][:].bitcast(F32)
+            first = g * ROUND % CHUNK
+            grad_words = grads[g * ROUND // CHUNK][:].bitcast(F32)
             grouped = stage.tile([P, ROUND, P, PACK], BF16, align_bytes=64)
             grouped_words = grouped[:].bitcast(F32)
             for b in range(ROUND // PAIR):
                 pair = slice(b * PAIR, (b + 1) * PAIR)
-                flipped = transpose_pair(nc, banks, grad_words[:, pair, 0 : DIM // 2], ident[:])
+                flipped = transpose_pair(
+                    nc,
+                    banks,
+                    grad_words[:, first + b * PAIR : first + (b + 1) * PAIR, 0 : DIM // 2],
+                    ident[:],
+                )
                 nc.scalar.copy(
                     out=grouped_words[:, pair, :, :],
                     in_=flipped[:].rearrange("p i h r -> p i r h"),
@@ -105,9 +116,14 @@ def tile_linear_sub_t_kernel(tc, pq, A, grad_out, out):
             return codes, scales
 
         def finish_round(g, codes, scales):
-            grad = grads[g]
-            result = results.tile([P, ROUND, 2 * DIM], F32)
-            nc.scalar.copy(out=result[:, :, 0:DIM], in_=grad[:, :, 0:DIM])
+            c = g * ROUND // CHUNK
+            first = g * ROUND % CHUNK
+            grad = grads[c]
+            result = results[c]
+            nc.scalar.copy(
+                out=result[:, first : first + ROUND, 0:DIM],
+                in_=grad[:, first : first + ROUND, 0:DIM],
+            )
             for i in range(ROUND):
                 tokens = slice(i * P, (i + 1) * P)
                 product = products.tile([P, DIM], F32)
@@ -121,12 +137,13 @@ def tile_linear_sub_t_kernel(tc, pq, A, grad_out, out):
                     stop=True,
                 )
                 nc.vector.tensor_tensor(
-                    out=result[:, i, DIM : 2 * DIM],
+                    out=result[:, first + i, DIM : 2 * DIM],
                     in0=product[:],
-                    in1=grad[:, i, DIM : 2 * DIM],
+                    in1=grad[:, first + i, DIM : 2 * DIM],
                     op=ADD,
                 )
-            nc.sync.dma_start(out=out_tiles[:, g * ROUND : (g + 1) * ROUND, :], in_=result[:])
+            if first + ROUND == CHUNK:
+                nc.sync.dma_start(out=out_tiles[:, c * CHUNK : (c + 1) * CHUNK, :], in_=result[:])
 
         ahead = quantise_round(0)
         for g in range(ROUNDS):

@@ -20,11 +20,15 @@ TILES = TOKENS // P
 PAIR = 2
 ROUND = 4
 ROUNDS = TILES // ROUND
-CHUNK = 8
-CHUNKS = TILES // CHUNK
+SPAN = 8
 
 FLOPS = 2 * TOKENS * DIM * DIM
 BYTES = TOKENS * 2 * DIM * 2 + DIM * DIM * 2 + TOKENS * 2 * DIM * 4
+
+
+def dma_spans():
+    half = SPAN // 2
+    return [(0, half), (half, SPAN)] + [(t, t + SPAN) for t in range(SPAN, TILES, SPAN)]
 
 
 def transpose_pair(nc, banks, words, ident):
@@ -45,28 +49,23 @@ def tile_linear_sub_t_kernel(tc, pq, A, grad_out, out):
     out_tiles = out.rearrange("(p t) f -> p t f", t=TILES)
 
     with ExitStack() as ctx:
-        const = ctx.enter_context(tc.tile_pool(name="const", bufs=1))
-        loaded = ctx.enter_context(tc.tile_pool(name="loaded", bufs=CHUNKS))
-        stored = ctx.enter_context(tc.tile_pool(name="stored", bufs=CHUNKS))
+        keep = ctx.enter_context(tc.tile_pool(name="keep", bufs=1))
         stage = ctx.enter_context(tc.tile_pool(name="stage", bufs=3))
         banks = ctx.enter_context(tc.psum_pool(name="banks", bufs=4))
         products = ctx.enter_context(tc.psum_pool(name="products", bufs=4))
 
-        a_rows = const.tile([P, PACK, DIM], BF16)
+        a_rows = keep.tile([P, PACK, DIM], BF16)
         nc.sync.dma_start(out=a_rows[:], in_=A.rearrange("(p j) d -> p j d", j=PACK))
-        grads = []
-        results = []
-        for c in range(CHUNKS):
-            grad = loaded.tile([P, CHUNK, 2 * DIM], BF16)
-            nc.sync.dma_start(out=grad[:], in_=grad_tiles[:, c * CHUNK : (c + 1) * CHUNK, :])
-            grads.append(grad)
-            result = stored.tile([P, CHUNK, 2 * DIM], F32)
-            results.append(result)
+        grad = keep.tile([P, TILES, 2 * DIM], BF16)
+        result = keep.tile([P, TILES, 2 * DIM], F32)
+        for first, end in dma_spans():
+            nc.sync.dma_start(out=grad[:, first:end, :], in_=grad_tiles[:, first:end, :])
+        grad_words = grad[:].bitcast(F32)
 
-        ident = const.tile([P, P], F32)
+        ident = keep.tile([P, P], F32)
         make_identity(nc, ident[:])
 
-        s_grouped = const.tile([P, DIM, PACK], BF16, align_bytes=64)
+        s_grouped = keep.tile([P, DIM, PACK], BF16, align_bytes=64)
         a_words = a_rows[:].bitcast(F32)
         for b in range(PACK // PAIR):
             c_range = slice(b * PAIR, (b + 1) * PAIR)
@@ -81,8 +80,8 @@ def tile_linear_sub_t_kernel(tc, pq, A, grad_out, out):
                 in1=flipped[:].bitcast(BF16).rearrange("p i h (q e) -> p q i h e", e=2),
                 op=ADD,
             )
-        s_codes = const.tile([P, DIM], U32, align_bytes=64)
-        s_scales = const.tile([P, DIM], U8, align_bytes=64)
+        s_codes = keep.tile([P, DIM], U32, align_bytes=64)
+        s_scales = keep.tile([P, DIM], U8, align_bytes=64)
         nc.vector.quantize_mx(
             out=s_codes[:].bitcast(E4M3_X4),
             scales=s_scales[:],
@@ -90,20 +89,15 @@ def tile_linear_sub_t_kernel(tc, pq, A, grad_out, out):
         )
 
         def quantise_round(g):
-            first = g * ROUND % CHUNK
-            grad_words = grads[g * ROUND // CHUNK][:].bitcast(F32)
             grouped = stage.tile([P, ROUND, P, PACK], BF16, align_bytes=64)
             grouped_words = grouped[:].bitcast(F32)
             for b in range(ROUND // PAIR):
-                pair = slice(b * PAIR, (b + 1) * PAIR)
+                t = g * ROUND + b * PAIR
                 flipped = transpose_pair(
-                    nc,
-                    banks,
-                    grad_words[:, first + b * PAIR : first + (b + 1) * PAIR, 0 : DIM // 2],
-                    ident[:],
+                    nc, banks, grad_words[:, t : t + PAIR, 0 : DIM // 2], ident[:]
                 )
                 nc.scalar.copy(
-                    out=grouped_words[:, pair, :, :],
+                    out=grouped_words[:, b * PAIR : (b + 1) * PAIR, :, :],
                     in_=flipped[:].rearrange("p i h r -> p i r h"),
                 )
             codes = stage.tile([P, ROUND * P], U32, align_bytes=64)
@@ -116,14 +110,8 @@ def tile_linear_sub_t_kernel(tc, pq, A, grad_out, out):
             return codes, scales
 
         def finish_round(g, codes, scales):
-            c = g * ROUND // CHUNK
-            first = g * ROUND % CHUNK
-            grad = grads[c]
-            result = results[c]
-            nc.scalar.copy(
-                out=result[:, first : first + ROUND, 0:DIM],
-                in_=grad[:, first : first + ROUND, 0:DIM],
-            )
+            t = g * ROUND
+            nc.scalar.copy(out=result[:, t : t + ROUND, 0:DIM], in_=grad[:, t : t + ROUND, 0:DIM])
             for i in range(ROUND):
                 tokens = slice(i * P, (i + 1) * P)
                 product = products.tile([P, DIM], F32)
@@ -137,17 +125,17 @@ def tile_linear_sub_t_kernel(tc, pq, A, grad_out, out):
                     stop=True,
                 )
                 nc.vector.tensor_tensor(
-                    out=result[:, first + i, DIM : 2 * DIM],
+                    out=result[:, t + i, DIM : 2 * DIM],
                     in0=product[:],
-                    in1=grad[:, first + i, DIM : 2 * DIM],
+                    in1=grad[:, t + i, DIM : 2 * DIM],
                     op=ADD,
                 )
-            if first + ROUND == CHUNK:
-                nc.sync.dma_start(out=out_tiles[:, c * CHUNK : (c + 1) * CHUNK, :], in_=result[:])
 
         ahead = quantise_round(0)
-        for g in range(ROUNDS):
-            codes, scales = ahead
-            if g + 1 < ROUNDS:
-                ahead = quantise_round(g + 1)
-            finish_round(g, codes, scales)
+        for first, end in dma_spans():
+            for g in range(first // ROUND, end // ROUND):
+                codes, scales = ahead
+                if g + 1 < ROUNDS:
+                    ahead = quantise_round(g + 1)
+                finish_round(g, codes, scales)
+            nc.sync.dma_start(out=out_tiles[:, first:end, :], in_=result[:, first:end, :])

@@ -1,7 +1,6 @@
 from contextlib import ExitStack
 
 import concourse.mybir as mybir
-from concourse.masks import make_identity
 
 BF16 = mybir.dt.bfloat16
 F32 = mybir.dt.float32
@@ -10,8 +9,10 @@ U8 = mybir.dt.uint8
 E4M3_X4 = mybir.dt.float8_e4m3fn_x4
 E5M2_X4 = mybir.dt.float8_e5m2_x4
 ADD = mybir.AluOpType.add
+IS_EQUAL = mybir.AluOpType.is_equal
 
 P = 128
+BLOCK = 32
 PACK = 4
 HALVES = 2
 DIM = P * PACK
@@ -29,6 +30,26 @@ BYTES = TOKENS * 2 * DIM * 2 + DIM * DIM * 2 + TOKENS * 2 * DIM * 4
 def dma_spans():
     half = SPAN // 2
     return [(0, half), (half, SPAN)] + [(t, t + SPAN) for t in range(SPAN, TILES, SPAN)]
+
+
+def make_identity_on_vector(nc, pool):
+    ramp = pool.tile([P, P], F32, align_bytes=64)
+    nc.vector.memset(ramp[:], 0.0)
+    bit = 1
+    while bit < P:
+        high = ramp[:].rearrange("p (a two b) -> p a two b", two=2, b=bit)[:, :, 1, :]
+        nc.vector.tensor_scalar(out=high, in0=high, scalar1=float(bit), scalar2=None, op0=ADD)
+        bit *= 2
+    rows = pool.tile([P, BLOCK], F32, align_bytes=64)
+    nc.vector.transpose(out=rows[:], in_=ramp[:, 0:BLOCK])
+    for first in range(BLOCK, P, BLOCK):
+        own = rows[first : first + BLOCK, :]
+        nc.vector.tensor_scalar(out=own, in0=own, scalar1=float(first), scalar2=None, op0=ADD)
+    ident = pool.tile([P, P], F32, align_bytes=64)
+    nc.vector.tensor_scalar(
+        out=ident[:], in0=ramp[:], scalar1=rows[:, 0:1], scalar2=None, op0=IS_EQUAL
+    )
+    return ident
 
 
 def transpose_pair(nc, banks, words, ident):
@@ -62,8 +83,7 @@ def tile_linear_sub_t_kernel(tc, pq, A, grad_out, out):
             nc.sync.dma_start(out=grad[:, first:end, :], in_=grad_tiles[:, first:end, :])
         grad_words = grad[:].bitcast(F32)
 
-        ident = keep.tile([P, P], F32)
-        make_identity(nc, ident[:])
+        ident = make_identity_on_vector(nc, keep)
 
         s_grouped = keep.tile([P, DIM, PACK], BF16, align_bytes=64)
         a_words = a_rows[:].bitcast(F32)

@@ -27,9 +27,8 @@ FLOPS = 2 * TOKENS * DIM * DIM
 BYTES = TOKENS * 2 * DIM * 2 + DIM * DIM * 2 + TOKENS * 2 * DIM * 4
 
 
-def dma_spans():
-    half = SPAN // 2
-    return [(0, half), (half, SPAN)] + [(t, t + SPAN) for t in range(SPAN, TILES, SPAN)]
+LOAD_SPANS = [(0, 8), (8, 16), (16, 32)]
+STORE_SPANS = [(t, t + SPAN) for t in range(0, TILES, SPAN)]
 
 
 def make_identity_on_vector(nc, pool):
@@ -79,7 +78,7 @@ def tile_linear_sub_t_kernel(tc, pq, A, grad_out, out):
         nc.sync.dma_start(out=a_rows[:], in_=A.rearrange("(p j) d -> p j d", j=PACK))
         grad = keep.tile([P, TILES, 2 * DIM], BF16)
         result = keep.tile([P, TILES, 2 * DIM], F32)
-        for first, end in dma_spans():
+        for first, end in LOAD_SPANS:
             nc.sync.dma_start(out=grad[:, first:end, :], in_=grad_tiles[:, first:end, :])
         grad_words = grad[:].bitcast(F32)
 
@@ -152,7 +151,7 @@ def tile_linear_sub_t_kernel(tc, pq, A, grad_out, out):
                 )
 
         ahead = quantise_round(0)
-        for first, end in dma_spans():
+        for first, end in STORE_SPANS:
             for g in range(first // ROUND, end // ROUND):
                 codes, scales = ahead
                 if g + 1 < ROUNDS:

@@ -27,8 +27,8 @@ FLOPS = 2 * TOKENS * DIM * DIM
 BYTES = TOKENS * 2 * DIM * 2 + DIM * DIM * 2 + TOKENS * 2 * DIM * 4
 
 
-LOAD_SPANS = [(0, 8), (8, 16), (16, 32)]
-STORE_SPANS = [(t, t + SPAN) for t in range(0, TILES, SPAN)]
+LOAD_SPANS = [(0, 4), (4, 16), (16, 32)]
+STORE_SPANS = [(0, 4), (4, 12), (12, 20), (20, 32)]
 
 
 def make_identity_on_vector(nc, pool):

from contextlib import ExitStack

import concourse.mybir as mybir

BF16 = mybir.dt.bfloat16
F32 = mybir.dt.float32
U32 = mybir.dt.uint32
U8 = mybir.dt.uint8
E4M3_X4 = mybir.dt.float8_e4m3fn_x4
E5M2_X4 = mybir.dt.float8_e5m2_x4
ADD = mybir.AluOpType.add
IS_EQUAL = mybir.AluOpType.is_equal

P = 128
BLOCK = 32
PACK = 4
HALVES = 2
DIM = P * PACK
TOKENS = 4096
TILES = TOKENS // P
PAIR = 2
ROUND = 4
ROUNDS = TILES // ROUND
SPAN = 8

FLOPS = 2 * TOKENS * DIM * DIM
BYTES = TOKENS * 2 * DIM * 2 + DIM * DIM * 2 + TOKENS * 2 * DIM * 4


LOAD_SPANS = [(0, 4), (4, 16), (16, 32)]
STORE_SPANS = [(0, 4), (4, 12), (12, 20), (20, 32)]


def make_identity_on_vector(nc, pool):
    ramp = pool.tile([P, P], F32, align_bytes=64)
    nc.vector.memset(ramp[:], 0.0)
    bit = 1
    while bit < P:
        high = ramp[:].rearrange("p (a two b) -> p a two b", two=2, b=bit)[:, :, 1, :]
        nc.vector.tensor_scalar(out=high, in0=high, scalar1=float(bit), scalar2=None, op0=ADD)
        bit *= 2
    rows = pool.tile([P, BLOCK], F32, align_bytes=64)
    nc.vector.transpose(out=rows[:], in_=ramp[:, 0:BLOCK])
    for first in range(BLOCK, P, BLOCK):
        own = rows[first : first + BLOCK, :]
        nc.vector.tensor_scalar(out=own, in0=own, scalar1=float(first), scalar2=None, op0=ADD)
    ident = pool.tile([P, P], F32, align_bytes=64)
    nc.vector.tensor_scalar(
        out=ident[:], in0=ramp[:], scalar1=rows[:, 0:1], scalar2=None, op0=IS_EQUAL
    )
    return ident


def transpose_pair(nc, banks, words, ident):
    flipped = banks.tile([P, PAIR, HALVES, P], F32)
    for i in range(PAIR):
        for h in range(HALVES):
            nc.tensor.transpose(
                out=flipped[:, i, h, :],
                in_=words[:, i, h : DIM // 2 : HALVES],
                identity=ident,
            )
    return flipped


def tile_linear_sub_t_kernel(tc, pq, A, grad_out, out):
    nc = tc.nc
    grad_tiles = grad_out.rearrange("(p t) f -> p t f", t=TILES)
    out_tiles = out.rearrange("(p t) f -> p t f", t=TILES)

    with ExitStack() as ctx:
        keep = ctx.enter_context(tc.tile_pool(name="keep", bufs=1))
        stage = ctx.enter_context(tc.tile_pool(name="stage", bufs=3))
        banks = ctx.enter_context(tc.psum_pool(name="banks", bufs=4))
        products = ctx.enter_context(tc.psum_pool(name="products", bufs=4))

        a_rows = keep.tile([P, PACK, DIM], BF16)
        nc.sync.dma_start(out=a_rows[:], in_=A.rearrange("(p j) d -> p j d", j=PACK))
        grad = keep.tile([P, TILES, 2 * DIM], BF16)
        result = keep.tile([P, TILES, 2 * DIM], F32)
        for first, end in LOAD_SPANS:
            nc.sync.dma_start(out=grad[:, first:end, :], in_=grad_tiles[:, first:end, :])
        grad_words = grad[:].bitcast(F32)

        ident = make_identity_on_vector(nc, keep)

        s_grouped = keep.tile([P, DIM, PACK], BF16, align_bytes=64)
        a_words = a_rows[:].bitcast(F32)
        for b in range(PACK // PAIR):
            c_range = slice(b * PAIR, (b + 1) * PAIR)
            flipped = transpose_pair(nc, banks, a_words[:, c_range, :], ident[:])
            nc.vector.tensor_tensor(
                out=s_grouped[:].rearrange("p (q c) (h e) -> p q c h e", c=PACK, e=2)[
                    :, :, c_range
                ],
                in0=a_rows[:].rearrange("p (h e) (q c) -> p q c h e", c=PACK, e=2)[
                    :, :, c_range
                ],
                in1=flipped[:].bitcast(BF16).rearrange("p i h (q e) -> p q i h e", e=2),
                op=ADD,
            )
        s_codes = keep.tile([P, DIM], U32, align_bytes=64)
        s_scales = keep.tile([P, DIM], U8, align_bytes=64)
        nc.vector.quantize_mx(
            out=s_codes[:].bitcast(E4M3_X4),
            scales=s_scales[:],
            in_=s_grouped[:].rearrange("p d j -> p (d j)"),
        )

        def quantise_round(g):
            grouped = stage.tile([P, ROUND, P, PACK], BF16, align_bytes=64)
            grouped_words = grouped[:].bitcast(F32)
            for b in range(ROUND // PAIR):
                t = g * ROUND + b * PAIR
                flipped = transpose_pair(
                    nc, banks, grad_words[:, t : t + PAIR, 0 : DIM // 2], ident[:]
                )
                nc.scalar.copy(
                    out=grouped_words[:, b * PAIR : (b + 1) * PAIR, :, :],
                    in_=flipped[:].rearrange("p i h r -> p i r h"),
                )
            codes = stage.tile([P, ROUND * P], U32, align_bytes=64)
            scales = stage.tile([P, ROUND * P], U8, align_bytes=64)
            nc.vector.quantize_mx(
                out=codes[:].bitcast(E5M2_X4),
                scales=scales[:],
                in_=grouped[:].rearrange("p i r j -> p (i r j)"),
            )
            return codes, scales

        def finish_round(g, codes, scales):
            t = g * ROUND
            nc.scalar.copy(out=result[:, t : t + ROUND, 0:DIM], in_=grad[:, t : t + ROUND, 0:DIM])
            for i in range(ROUND):
                tokens = slice(i * P, (i + 1) * P)
                product = products.tile([P, DIM], F32)
                nc.tensor.matmul_mx(
                    out=product[:],
                    lhsT=codes[:, tokens].bitcast(E5M2_X4),
                    lhsT_scale=scales[:, tokens],
                    rhs=s_codes[:].bitcast(E4M3_X4),
                    rhs_scale=s_scales[:],
                    start=True,
                    stop=True,
                )
                nc.vector.tensor_tensor(
                    out=result[:, t + i, DIM : 2 * DIM],
                    in0=product[:],
                    in1=grad[:, t + i, DIM : 2 * DIM],
                    op=ADD,
                )

        ahead = quantise_round(0)
        for first, end in STORE_SPANS:
            for g in range(first // ROUND, end // ROUND):
                codes, scales = ahead
                if g + 1 < ROUNDS:
                    ahead = quantise_round(g + 1)
                finish_round(g, codes, scales)
            nc.sync.dma_start(out=out_tiles[:, first:end, :], in_=result[:, first:end, :])
